import numpy as np
import ml_dtypes


def mxq(x, axis, fmt="e4m3"):
    dtype, down = {"e4m3": (ml_dtypes.float8_e4m3fn, 7), "e5m2": (ml_dtypes.float8_e5m2, 14)}[fmt]
    v = np.moveaxis(np.asarray(x, np.float32).astype(ml_dtypes.bfloat16).astype(np.float64), axis, -1)
    blocks = v.reshape(v.shape[:-1] + (-1, 32))
    amax = np.abs(blocks).max(-1, keepdims=True)
    byte = np.maximum(np.where(amax > 0, np.frexp(amax)[1] - 1 + 127, 0) - down, 1)
    scale = np.exp2(byte - 127.0)
    codes = (blocks / scale).astype(np.float32).astype(dtype).astype(np.float64)
    return np.moveaxis((codes * scale).reshape(v.shape), -1, axis)


WIDE = False


def mx_kscale(k):
    if not WIDE:
        return np.ones(k)
    levels = np.array([10, -10, 5, -5, 0])
    if k % 512:
        return np.exp2(np.random.permutation(np.resize(levels, k // 32))).repeat(32)
    a = np.empty((k // 512, 16))
    for p in range(k // 512):
        a[p, :8] = np.random.permutation(np.resize(levels, 8))
        for g in range(8):
            far = levels[np.abs(levels - a[p, g]) >= 10]
            a[p, g + 8] = far[np.random.randint(len(far))]
    return np.exp2(a.ravel()).repeat(32)


BF16 = ml_dtypes.bfloat16


def bf(x):
    return np.asarray(x, np.float32).astype(BF16)


def f64(x):
    return np.asarray(x).astype(np.float64)


B, T, C, H, D, R = 1, 1024, 2048, 16, 128, 512
EPS = 1e-6
THETA = 10000.0


def rmsnorm(v, w):
    var = np.mean(v * v, axis=-1, keepdims=True)
    return v * (1.0 / np.sqrt(var + EPS)) * w


def rope(v, cos, sin):
    re, im = v[..., 0::2], v[..., 1::2]
    c, s = cos[None, :, None, :], sin[None, :, None, :]
    return np.stack([re * c - im * s, re * s + im * c], axis=-1).reshape(v.shape)


def setup_inputs():
    s, t = mx_kscale(C), mx_kscale(R)
    ang = np.outer(np.arange(T), 1.0 / THETA ** (np.arange(0, D, 2) / D))
    return {"x": bf(np.random.standard_normal((B, T, C)) * s),
            "w_kv_down": bf(np.random.standard_normal((R, C)) / np.sqrt(C) / s[None, :] * t[:, None]),
            "w_kv_up": bf(np.random.standard_normal((2 * H * D, R)) / np.sqrt(R) / t[None, :]),
            "k_norm_w": bf(1.0 + 0.1 * np.random.standard_normal(D)),
            "freqs_cos": bf(np.cos(ang)), "freqs_sin": bf(np.sin(ang))}


def reference(x, w_kv_down, w_kv_up, k_norm_w, freqs_cos, freqs_sin):
    latent = mxq(f64(x), 2, "e4m3") @ mxq(f64(w_kv_down), 1, "e4m3").T
    kv = (mxq(latent, 2, "e4m3") @ mxq(f64(w_kv_up), 1, "e4m3").T).reshape(B, T, 2, H, D)
    xk, xv = kv[:, :, 0], kv[:, :, 1]
    return rope(rmsnorm(xk, f64(k_norm_w)), f64(freqs_cos), f64(freqs_sin)), xv

@@ -1,0 +1,317 @@
+from contextlib import ExitStack
+
+import concourse.mybir as mybir
+from concourse.masks import make_identity
+
+F32 = mybir.dt.float32
+BF16 = mybir.dt.bfloat16
+U32 = mybir.dt.uint32
+U8 = mybir.dt.uint8
+FP8X4 = mybir.dt.float8_e4m3fn_x4
+ALU = mybir.AluOpType
+ACT = mybir.ActivationFunctionType
+
+P = 128
+PACK = 4
+K_PASS = P * PACK
+BANK = 512
+
+TOKENS, C, R, HEADS, D = 1024, 2048, 512, 16, 128
+EPS = 1e-6
+HALF = D // 2
+TOKEN_TILES = TOKENS // P
+C_PASSES = C // K_PASS
+R_GROUPS = R // P
+HEADS_PER_BANK = BANK // D
+VECTOR_VALUES_STEP = 2
+KEYS, VALUES = 0, 1
+BLOCKS_PER_CHUNK = HEADS * D // 2 // P
+BANKS_PER_CHUNK = BLOCKS_PER_CHUNK * P // BANK
+
+FLOPS = 2 * TOKENS * C * R + 2 * TOKENS * R * 2 * HEADS * D
+
+
+def transpose_blocks(nc, psum, grouped, matrix, blocks):
+    grouped_words = grouped.bitcast(F32).rearrange("p (a r u) -> p a r u", r=P, u=2)
+    for pair in range(len(blocks) // 2):
+        bank = psum.tile([P, 2, 2, P], F32, tag="bank")
+        for a in range(2):
+            words = blocks[2 * pair + a].bitcast(F32)
+            for u in range(2):
+                nc.tensor.transpose(bank[:, a, u, :], words[:, u::2], matrix)
+        copy_out = nc.vector.tensor_copy if pair % 4 == 3 else nc.scalar.copy
+        copy_out(
+            out=grouped_words[:, 2 * pair : 2 * pair + 2, :, :],
+            in_=bank[:].rearrange("p a u r -> p a r u"),
+        )
+
+
+def tile_mla_pa_kernel(
+    tc, x, w_kv_down, w_kv_up, k_norm_w, freqs_cos, freqs_sin, out_0, out_1
+):
+    nc = tc.nc
+    x_view = x.flatten_outer_dims().rearrange("(p i) c -> p i c", i=TOKEN_TILES)
+    k_out_view = out_0.flatten_outer_dims().rearrange(
+        "(p i h) d -> p i (h d)", i=TOKEN_TILES, h=HEADS
+    )
+    v_out_view = out_1.flatten_outer_dims().rearrange(
+        "(p i h) d -> p i (h d)", i=TOKEN_TILES, h=HEADS
+    )
+
+    with ExitStack() as stack:
+        stack.enter_context(tc.manual_schedule())
+        keep = stack.enter_context(tc.tile_pool(name="keep", bufs=1))
+        weight_stage = stack.enter_context(tc.tile_pool(name="weight_stage", bufs=3))
+        token_stage = stack.enter_context(tc.tile_pool(name="token_stage", bufs=2))
+        stats = stack.enter_context(tc.tile_pool(name="stats", bufs=4))
+        results = stack.enter_context(tc.tile_pool(name="results", bufs=3))
+        psum = stack.enter_context(tc.psum_pool(name="psum", bufs=8))
+
+        wd_rows = w_kv_down.rearrange("(q a b) c -> a q b c", a=2, b=2)
+        wd_raw = []
+        for a in range(2):
+            wd_half = keep.tile([P, 2, C], BF16, name="wd_raw%d" % a)
+            nc.sync.dma_start(out=wd_half[:], in_=wd_rows[a])
+            wd_raw.append(wd_half)
+        x_raw = []
+        for pair in range(TOKEN_TILES // 2):
+            x_raw.append(keep.tile([P, 2, C], BF16, name="x_raw%d" % pair))
+        nc.sync.dma_start(out=x_raw[0][:], in_=x_view[:, 0:2, :])
+        wu_blocks = w_kv_up.rearrange("(n p) r -> p n r", p=P)
+        wu_raw = {}
+        for half in range(2):
+            for kind in (KEYS, VALUES):
+                first_block = (2 * kind + half) * BLOCKS_PER_CHUNK
+                wu_part = keep.tile([P, BLOCKS_PER_CHUNK, R], BF16, name="wu_raw%d%d" % (kind, half))
+                nc.sync.dma_start(
+                    out=wu_part[:], in_=wu_blocks[:, first_block : first_block + BLOCKS_PER_CHUNK, :]
+                )
+                wu_raw[(kind, half)] = wu_part
+        for pair in range(1, TOKEN_TILES // 2):
+            nc.sync.dma_start(out=x_raw[pair][:], in_=x_view[:, 2 * pair : 2 * pair + 2, :])
+
+        cos_bf = keep.tile([P, TOKEN_TILES, HALF], BF16, name="cos_bf")
+        sin_bf = keep.tile([P, TOKEN_TILES, HALF], BF16, name="sin_bf")
+        gain_bf = keep.tile([P, HALF, 2], BF16, name="gain_bf")
+        nc.scalar.dma_start(out=cos_bf[:], in_=freqs_cos.rearrange("(p i) j -> p i j", i=TOKEN_TILES))
+        nc.scalar.dma_start(out=sin_bf[:], in_=freqs_sin.rearrange("(p i) j -> p i j", i=TOKEN_TILES))
+        nc.scalar.dma_start(
+            out=gain_bf[:].rearrange("p j e -> p (j e)"), in_=k_norm_w.partition_broadcast(P)
+        )
+
+        one = keep.tile([P, 1], F32, name="one")
+        nc.vector.memset(one[:], 1.0)
+        nc.scalar.activation(out=one[:], in_=one[:], func=ACT.Abs_reciprocal_sqrt)
+        ident = keep.tile([P, P], F32, name="ident")
+        make_identity(nc, ident[:])
+        split_pairs = keep.tile([P, 2, HALF], F32, name="split_pairs")
+        nc.vector.tensor_copy(out=split_pairs[:], in_=ident[:].rearrange("p (j e) -> p e j", e=2))
+
+        rope_table = keep.tile([P, TOKEN_TILES, 2, HALF, 2], F32, name="rope_table")
+        neg_gain = keep.tile([P, HALF, 2], BF16, name="neg_gain")
+        nc.gpsimd.tensor_scalar(
+            out=neg_gain[:], in0=gain_bf[:], scalar1=-1.0, scalar2=0.0, op0=ALU.mult, op1=ALU.add
+        )
+        factors = [
+            (0, 0, cos_bf, gain_bf),
+            (0, 1, sin_bf, gain_bf),
+            (1, 0, sin_bf, neg_gain),
+            (1, 1, cos_bf, gain_bf),
+        ]
+        for e, w, angle, gain in factors:
+            nc.gpsimd.tensor_tensor(
+                out=rope_table[:, :, e, :, w],
+                in0=angle[:],
+                in1=gain[:, :, e].unsqueeze(1).to_broadcast([P, TOKEN_TILES, HALF]),
+                op=ALU.mult,
+            )
+
+        def quantise(grouped, codes, scales):
+            nc.vector.quantize_mx(out=codes.bitcast(FP8X4), scales=scales, in_=grouped)
+
+        def transpose_weight(blocks, matrix):
+            grouped = weight_stage.tile([P, len(blocks) * K_PASS], BF16, tag="grouped", align_bytes=64)
+            transpose_blocks(nc, psum, grouped[:], matrix, blocks)
+            return grouped
+
+        wd_codes = keep.tile([P, C_PASSES, R_GROUPS, P], U32, name="wd_codes", align_bytes=64)
+        wd_scales = keep.tile([P, C_PASSES, R_GROUPS, P], U8, name="wd_scales", align_bytes=64)
+
+        def transpose_wd(first_pass):
+            blocks = [
+                wd_raw[t // 2][:, t % 2, g * K_PASS : (g + 1) * K_PASS]
+                for g in range(first_pass, first_pass + 2)
+                for t in range(R_GROUPS)
+            ]
+            return transpose_weight(blocks, ident[:])
+
+        def quantise_wd(first_pass, grouped):
+            passes = slice(first_pass, first_pass + 2)
+            quantise(
+                grouped[:],
+                wd_codes[:, passes, :, :].rearrange("p g t q -> p (g t q)"),
+                wd_scales[:, passes, :, :].rearrange("p g t q -> p (g t q)"),
+            )
+
+        wu_mx = {}
+
+        def transpose_wu(kind, half):
+            blocks = [wu_raw[(kind, half)][:, n, :] for n in range(BLOCKS_PER_CHUNK)]
+            matrix = split_pairs[:].rearrange("p e j -> p (e j)") if kind == KEYS else ident[:]
+            return transpose_weight(blocks, matrix)
+
+        def quantise_wu(kind, half, grouped):
+            columns = BLOCKS_PER_CHUNK * P
+            wu_codes = keep.tile([P, columns], U32, name="wu_codes%d%d" % (kind, half), align_bytes=64)
+            wu_scales = keep.tile([P, columns], U8, name="wu_scales%d%d" % (kind, half), align_bytes=64)
+            quantise(grouped[:], wu_codes[:], wu_scales[:])
+            wu_mx[(kind, half)] = (wu_codes, wu_scales)
+
+        x_grouped, x_mx, lat_banks, lat_grouped, lat_mx = {}, {}, {}, {}, {}
+
+        def stage_transpose_x(n):
+            x_grouped[n] = token_stage.tile(
+                [P, C_PASSES * K_PASS], BF16, name="x_grouped", tag="x_grouped", align_bytes=64
+            )
+            blocks = [x_raw[n // 2][:, n % 2, g * K_PASS : (g + 1) * K_PASS] for g in range(C_PASSES)]
+            transpose_blocks(nc, psum, x_grouped[n][:], ident[:], blocks)
+
+        def stage_quantise_x(n):
+            x_codes = token_stage.tile([P, C_PASSES, P], U32, tag="x_codes", align_bytes=64)
+            x_scales = token_stage.tile([P, C_PASSES, P], U8, tag="x_scales", align_bytes=64)
+            quantise(
+                x_grouped[n][:],
+                x_codes[:].rearrange("p g r -> p (g r)"),
+                x_scales[:].rearrange("p g r -> p (g r)"),
+            )
+            x_mx[n] = (x_codes, x_scales)
+
+        def stage_latent(n):
+            x_codes, x_scales = x_mx[n]
+            lat_bank = psum.tile([P, R_GROUPS, P], F32, tag="bank")
+            for t in range(R_GROUPS):
+                for g in range(C_PASSES):
+                    nc.tensor.matmul_mx(
+                        out=lat_bank[:, t, :],
+                        lhsT=wd_codes[:, g, t, :].bitcast(FP8X4),
+                        lhsT_scale=wd_scales[:, g, t, :],
+                        rhs=x_codes[:, g, :].bitcast(FP8X4),
+                        rhs_scale=x_scales[:, g, :],
+                        start=(g == 0),
+                        stop=(g == C_PASSES - 1),
+                    )
+            lat_banks[n] = lat_bank
+
+        def stage_round_latent(n):
+            lat_grouped[n] = token_stage.tile(
+                [P, P, R_GROUPS], BF16, name="lat_grouped", tag="lat_grouped", align_bytes=64
+            )
+            nc.vector.tensor_copy(out=lat_grouped[n][:], in_=lat_banks[n][:].rearrange("p t r -> p r t"))
+
+        def stage_quantise_latent(n):
+            lat_codes = token_stage.tile([P, P], U32, tag="lat_codes", align_bytes=64)
+            lat_scales = token_stage.tile([P, P], U8, tag="lat_scales", align_bytes=64)
+            quantise(lat_grouped[n][:].rearrange("p r t -> p (r t)"), lat_codes[:], lat_scales[:])
+            lat_mx[n] = (lat_codes, lat_scales)
+
+        wd_first = transpose_wd(0)
+        wd_second = transpose_wd(2)
+        quantise_wd(0, wd_first)
+        stage_transpose_x(0)
+        stage_transpose_x(1)
+        quantise_wd(2, wd_second)
+        keys_low = transpose_wu(KEYS, 0)
+        stage_quantise_x(0)
+        stage_quantise_x(1)
+        values_low = transpose_wu(VALUES, 0)
+        quantise_wu(KEYS, 0, keys_low)
+        stage_latent(0)
+        stage_latent(1)
+        quantise_wu(VALUES, 0, values_low)
+        stage_round_latent(0)
+        stage_round_latent(1)
+        stage_quantise_latent(0)
+        keys_high = transpose_wu(KEYS, 1)
+        values_high = transpose_wu(VALUES, 1)
+        quantise_wu(KEYS, 1, keys_high)
+        quantise_wu(VALUES, 1, values_high)
+
+        def project(bank, n, kind, step):
+            lat_codes, lat_scales = lat_mx[n]
+            wu_codes, wu_scales = wu_mx[(kind, step // BANKS_PER_CHUNK)]
+            columns = slice((step % BANKS_PER_CHUNK) * BANK, (step % BANKS_PER_CHUNK + 1) * BANK)
+            nc.tensor.matmul_mx(
+                out=bank,
+                lhsT=lat_codes[:].bitcast(FP8X4),
+                lhsT_scale=lat_scales[:],
+                rhs=wu_codes[:, columns].bitcast(FP8X4),
+                rhs_scale=wu_scales[:, columns],
+                start=True,
+                stop=True,
+            )
+
+        def store_two_banks(out_view, i, step, result):
+            columns = slice((step - 1) * BANK, (step + 1) * BANK)
+            nc.sync.dma_start(out=out_view[:, i, columns], in_=result[:, columns])
+
+        def add_products(i, step, products, k_rot):
+            heads = slice(step * HEADS_PER_BANK, (step + 1) * HEADS_PER_BANK)
+            nc.gpsimd.tensor_tensor(
+                out=k_rot[:, heads, :], in0=products[:, :, 0, :], in1=products[:, :, 1, :], op=ALU.add
+            )
+            if step % 2 == 1:
+                store_two_banks(k_out_view, i, step, k_rot[:].rearrange("p h d -> p (h d)"))
+
+        def project_step(i, step, k_rot, v_sb):
+            k_bank = psum.tile([P, HEADS_PER_BANK, D], F32, tag="bank")
+            project(k_bank[:].rearrange("p h d -> p (h d)"), i, KEYS, step)
+            v_bank = psum.tile([P, BANK], F32, tag="bank")
+            project(v_bank[:], i, VALUES, step)
+
+            squares = stats.tile([P, HEADS_PER_BANK, D], BF16, tag="squares", bufs=2)
+            sumsq = stats.tile([P, HEADS_PER_BANK], F32, tag="sumsq")
+            rstd = stats.tile([P, HEADS_PER_BANK], F32, tag="rstd")
+            for h in range(HEADS_PER_BANK):
+                nc.scalar.activation(
+                    out=squares[:, h, :],
+                    in_=k_bank[:, h, :],
+                    func=ACT.Square,
+                    accum_out=sumsq[:, h : h + 1],
+                )
+            if step != VECTOR_VALUES_STEP:
+                nc.scalar.copy(out=v_sb[:, step * BANK : (step + 1) * BANK], in_=v_bank[:])
+            nc.scalar.activation(
+                out=rstd[:], in_=sumsq[:], func=ACT.Abs_reciprocal_sqrt, scale=1.0 / D, bias=EPS
+            )
+
+            products = results.tile([P, HEADS_PER_BANK, 2, D], F32, tag="products", bufs=4)
+            for h in range(HEADS_PER_BANK):
+                nc.vector.scalar_tensor_tensor(
+                    out=products[:, h, :, :].rearrange("p e (j w) -> p (e j) w", w=2),
+                    in0=k_bank[:, h, :].unsqueeze(2).to_broadcast([P, D, 2]),
+                    scalar=rstd[:, h : h + 1],
+                    in1=rope_table[:, i, :, :, :].rearrange("p e j w -> p (e j) w"),
+                    op0=ALU.mult,
+                    op1=ALU.mult,
+                )
+            add_products(i, step, products, k_rot)
+            if step == VECTOR_VALUES_STEP:
+                nc.vector.tensor_copy(out=v_sb[:, step * BANK : (step + 1) * BANK], in_=v_bank[:])
+            if step % 2 == 1:
+                store_two_banks(v_out_view, i, step, v_sb[:])
+
+        for i in range(TOKEN_TILES):
+            k_rot = results.tile([P, HEADS, D], F32, tag="k_rot")
+            v_sb = results.tile([P, HEADS * D], F32, tag="v_sb")
+            project_step(i, 0, k_rot, v_sb)
+            if i + 2 < TOKEN_TILES:
+                stage_transpose_x(i + 2)
+                stage_quantise_x(i + 2)
+            if i + 1 < TOKEN_TILES:
+                stage_quantise_latent(i + 1)
+            project_step(i, 1, k_rot, v_sb)
+            project_step(i, 2, k_rot, v_sb)
+            project_step(i, 3, k_rot, v_sb)
+            if i + 2 < TOKEN_TILES:
+                stage_latent(i + 2)
+                stage_round_latent(i + 2)

@@ -23,27 +23,12 @@ TOKEN_TILES = TOKENS // P
 C_PASSES = C // K_PASS
 R_GROUPS = R // P
 HEADS_PER_BANK = BANK // D
-VECTOR_VALUES_STEP = 2
+CHUNKS = HEADS // HEADS_PER_BANK
 KEYS, VALUES = 0, 1
-BLOCKS_PER_CHUNK = HEADS * D // 2 // P
-BANKS_PER_CHUNK = BLOCKS_PER_CHUNK * P // BANK
 
 FLOPS = 2 * TOKENS * C * R + 2 * TOKENS * R * 2 * HEADS * D
 
-
-def transpose_blocks(nc, psum, grouped, matrix, blocks):
-    grouped_words = grouped.bitcast(F32).rearrange("p (a r u) -> p a r u", r=P, u=2)
-    for pair in range(len(blocks) // 2):
-        bank = psum.tile([P, 2, 2, P], F32, tag="bank")
-        for a in range(2):
-            words = blocks[2 * pair + a].bitcast(F32)
-            for u in range(2):
-                nc.tensor.transpose(bank[:, a, u, :], words[:, u::2], matrix)
-        copy_out = nc.vector.tensor_copy if pair % 4 == 3 else nc.scalar.copy
-        copy_out(
-            out=grouped_words[:, 2 * pair : 2 * pair + 2, :, :],
-            in_=bank[:].rearrange("p a u r -> p a r u"),
-        )
+DOWN, TOKEN, UP = "down", "token", "up"
 
 
 def tile_mla_pa_kernel(
@@ -51,150 +36,142 @@ def tile_mla_pa_kernel(
 ):
     nc = tc.nc
     x_view = x.flatten_outer_dims().rearrange("(p i) c -> p i c", i=TOKEN_TILES)
-    k_out_view = out_0.flatten_outer_dims().rearrange(
-        "(p i h) d -> p i (h d)", i=TOKEN_TILES, h=HEADS
-    )
-    v_out_view = out_1.flatten_outer_dims().rearrange(
-        "(p i h) d -> p i (h d)", i=TOKEN_TILES, h=HEADS
-    )
+    wd_view = w_kv_down.rearrange("(q t) c -> q t c", t=R_GROUPS)
+    wu_view = w_kv_up.rearrange("(n g q e) r -> n q g e r", g=2, q=P, e=2)
+    k_out_view = out_0.flatten_outer_dims().rearrange("(p i h) d -> p i (h d)", i=TOKEN_TILES, h=HEADS)
+    v_out_view = out_1.flatten_outer_dims().rearrange("(p i h) d -> p i (h d)", i=TOKEN_TILES, h=HEADS)
 
     with ExitStack() as stack:
         stack.enter_context(tc.manual_schedule())
         keep = stack.enter_context(tc.tile_pool(name="keep", bufs=1))
-        weight_stage = stack.enter_context(tc.tile_pool(name="weight_stage", bufs=3))
-        token_stage = stack.enter_context(tc.tile_pool(name="token_stage", bufs=2))
+        stage = stack.enter_context(tc.tile_pool(name="stage", bufs=3))
         stats = stack.enter_context(tc.tile_pool(name="stats", bufs=4))
-        results = stack.enter_context(tc.tile_pool(name="results", bufs=3))
+        results = stack.enter_context(tc.tile_pool(name="results", bufs=8))
         psum = stack.enter_context(tc.psum_pool(name="psum", bufs=8))
 
-        wd_rows = w_kv_down.rearrange("(q a b) c -> a q b c", a=2, b=2)
-        wd_raw = []
-        for a in range(2):
-            wd_half = keep.tile([P, 2, C], BF16, name="wd_raw%d" % a)
-            nc.sync.dma_start(out=wd_half[:], in_=wd_rows[a])
-            wd_raw.append(wd_half)
-        x_raw = []
-        for pair in range(TOKEN_TILES // 2):
-            x_raw.append(keep.tile([P, 2, C], BF16, name="x_raw%d" % pair))
-        nc.sync.dma_start(out=x_raw[0][:], in_=x_view[:, 0:2, :])
-        wu_blocks = w_kv_up.rearrange("(n p) r -> p n r", p=P)
-        wu_raw = {}
-        for half in range(2):
-            for kind in (KEYS, VALUES):
-                first_block = (2 * kind + half) * BLOCKS_PER_CHUNK
-                wu_part = keep.tile([P, BLOCKS_PER_CHUNK, R], BF16, name="wu_raw%d%d" % (kind, half))
+        raw = {}
+
+        def load(unit):
+            kind, a, b = unit
+            tile = stage.tile([P, C], BF16, name="raw", tag="raw", bufs=14)
+            if kind == DOWN:
+                nc.sync.dma_start(out=tile[:], in_=wd_view[:, a, :])
+            elif kind == TOKEN and a == 0:
+                for g in range(C_PASSES):
+                    nc.sync.dma_start(out=tile[:, g * K_PASS : (g + 1) * K_PASS], in_=x_view[:, a, g * K_PASS : (g + 1) * K_PASS])
+            elif kind == TOKEN:
+                nc.sync.dma_start(out=tile[:], in_=x_view[:, a, :])
+            else:
                 nc.sync.dma_start(
-                    out=wu_part[:], in_=wu_blocks[:, first_block : first_block + BLOCKS_PER_CHUNK, :]
+                    out=tile[:].rearrange("p (g e r) -> p g e r", g=2, e=2), in_=wu_view[a * CHUNKS + b]
                 )
-                wu_raw[(kind, half)] = wu_part
-        for pair in range(1, TOKEN_TILES // 2):
-            nc.sync.dma_start(out=x_raw[pair][:], in_=x_view[:, 2 * pair : 2 * pair + 2, :])
+            raw[unit] = tile
 
-        cos_bf = keep.tile([P, TOKEN_TILES, HALF], BF16, name="cos_bf")
-        sin_bf = keep.tile([P, TOKEN_TILES, HALF], BF16, name="sin_bf")
-        gain_bf = keep.tile([P, HALF, 2], BF16, name="gain_bf")
-        nc.scalar.dma_start(out=cos_bf[:], in_=freqs_cos.rearrange("(p i) j -> p i j", i=TOKEN_TILES))
-        nc.scalar.dma_start(out=sin_bf[:], in_=freqs_sin.rearrange("(p i) j -> p i j", i=TOKEN_TILES))
-        nc.scalar.dma_start(
-            out=gain_bf[:].rearrange("p j e -> p (j e)"), in_=k_norm_w.partition_broadcast(P)
-        )
-
+        down = [(DOWN, t, 0) for t in range(R_GROUPS)]
+        token = [(TOKEN, n, 0) for n in range(TOKEN_TILES)]
+        up = [[(UP, kind, chunk) for kind in (KEYS, VALUES)] for chunk in range(CHUNKS)]
+        prologue = [token[0]] + down + [token[1]] + up[0] + up[1]
+        planned = [(up[2][0], 0), (token[2], 0), (up[2][1], 1), (token[3], 1), (up[3][0], 3), (up[3][1], 4)]
+        planned += [(token[4], 7), (token[5], 8), (token[6], 12), (token[7], 13)]
+        gain_row = keep.tile([P, D], BF16, name="gain_row")
+        nc.vector.memset(gain_row[:], 0.0)
+        ones = keep.tile([P, P], BF16, name="ones")
+        nc.vector.memset(ones[:], 1.0)
         one = keep.tile([P, 1], F32, name="one")
         nc.vector.memset(one[:], 1.0)
         nc.scalar.activation(out=one[:], in_=one[:], func=ACT.Abs_reciprocal_sqrt)
+
+        cos_bf = keep.tile([P, TOKEN_TILES, HALF], BF16, name="cos_bf")
+        sin_bf = keep.tile([P, TOKEN_TILES, HALF], BF16, name="sin_bf")
+        for n, unit in enumerate(prologue + [unit for unit, s in planned]):
+            load(unit)
+            if n == 4:
+                nc.sync.dma_start(out=cos_bf[:], in_=freqs_cos.rearrange("(p i) j -> p i j", i=TOKEN_TILES))
+                nc.sync.dma_start(out=sin_bf[:], in_=freqs_sin.rearrange("(p i) j -> p i j", i=TOKEN_TILES))
+                nc.sync.dma_start(out=gain_row[0:1, :], in_=k_norm_w.unsqueeze(0))
+
         ident = keep.tile([P, P], F32, name="ident")
         make_identity(nc, ident[:])
-        split_pairs = keep.tile([P, 2, HALF], F32, name="split_pairs")
-        nc.vector.tensor_copy(out=split_pairs[:], in_=ident[:].rearrange("p (j e) -> p e j", e=2))
 
         rope_table = keep.tile([P, TOKEN_TILES, 2, HALF, 2], F32, name="rope_table")
-        neg_gain = keep.tile([P, HALF, 2], BF16, name="neg_gain")
-        nc.gpsimd.tensor_scalar(
-            out=neg_gain[:], in0=gain_bf[:], scalar1=-1.0, scalar2=0.0, op0=ALU.mult, op1=ALU.add
-        )
-        factors = [
-            (0, 0, cos_bf, gain_bf),
-            (0, 1, sin_bf, gain_bf),
-            (1, 0, sin_bf, neg_gain),
-            (1, 1, cos_bf, gain_bf),
-        ]
-        for e, w, angle, gain in factors:
-            nc.gpsimd.tensor_tensor(
-                out=rope_table[:, :, e, :, w],
-                in0=angle[:],
-                in1=gain[:, :, e].unsqueeze(1).to_broadcast([P, TOKEN_TILES, HALF]),
-                op=ALU.mult,
+        gain = keep.tile([P, HALF, 2], F32, name="gain")
+        neg_gain = keep.tile([P, HALF, 2], F32, name="neg_gain")
+
+        def spread_gain():
+            bank = psum.tile([P, BANK], F32, tag="bank")
+            nc.tensor.matmul(bank[:, 0:D], lhsT=ones[:], rhs=gain_row[:], start=True, stop=True)
+            nc.scalar.copy(out=gain[:].rearrange("p j e -> p (j e)"), in_=bank[:, 0:D])
+            nc.gpsimd.tensor_scalar(
+                out=neg_gain[:], in0=gain[:], scalar1=-1.0, scalar2=0.0, op0=ALU.mult, op1=ALU.add
             )
 
-        def quantise(grouped, codes, scales):
-            nc.vector.quantize_mx(out=codes.bitcast(FP8X4), scales=scales, in_=grouped)
+        def make_rope_table(tiles):
+            count = tiles.stop - tiles.start
+            for e, w, angle, factor in [
+                (0, 0, cos_bf, gain),
+                (0, 1, sin_bf, gain),
+                (1, 0, sin_bf, neg_gain),
+                (1, 1, cos_bf, gain),
+            ]:
+                nc.gpsimd.tensor_tensor(
+                    out=rope_table[:, tiles, e, :, w],
+                    in0=angle[:, tiles, :],
+                    in1=factor[:, :, e].unsqueeze(1).to_broadcast([P, count, HALF]),
+                    op=ALU.mult,
+                )
 
-        def transpose_weight(blocks, matrix):
-            grouped = weight_stage.tile([P, len(blocks) * K_PASS], BF16, tag="grouped", align_bytes=64)
-            transpose_blocks(nc, psum, grouped[:], matrix, blocks)
-            return grouped
+        grouped, codes, scales = {}, {}, {}
 
-        wd_codes = keep.tile([P, C_PASSES, R_GROUPS, P], U32, name="wd_codes", align_bytes=64)
-        wd_scales = keep.tile([P, C_PASSES, R_GROUPS, P], U8, name="wd_scales", align_bytes=64)
+        def transpose(unit, engines):
+            words = raw[unit][:].bitcast(F32).rearrange("p (b w) -> p b w", b=4)
+            tile = stage.tile([P, 4 * P * PACK], BF16, name="grouped", tag="grouped", align_bytes=64, bufs=5)
+            grouped_words = tile[:].bitcast(F32).rearrange("p (b r u) -> p b r u", b=4, u=2)
+            for pair in range(2):
+                bank = psum.tile([P, 2, 2, P], F32, tag="bank")
+                for a in range(2):
+                    for u in range(2):
+                        nc.tensor.transpose(bank[:, a, u, :], words[:, 2 * pair + a, u::2], ident[:])
+                copy_out = nc.vector.tensor_copy if engines[pair] == "v" else nc.scalar.copy
+                words_out = grouped_words[:, 2 * pair : 2 * pair + 2, :, :]
+                if unit[0] != UP:
+                    copy_out(out=words_out, in_=bank[:].rearrange("p a u r -> p a r u"))
+                elif unit[1] == VALUES:
+                    copy_out(
+                        out=words_out.rearrange("p a r u -> p (a r u)").rearrange("p (r a u) -> p r a u", a=2, u=2),
+                        in_=bank[:].rearrange("p a u r -> p r a u"),
+                    )
+                else:
+                    for head in range(2):
+                        rows = slice(head * HALF, (head + 1) * HALF)
+                        copy_out(
+                            out=words_out[:, head, :, :].rearrange("p (a j) u -> p a j u", a=2),
+                            in_=bank[:, :, :, rows].rearrange("p a u j -> p a j u"),
+                        )
+            grouped[unit] = tile
 
-        def transpose_wd(first_pass):
-            blocks = [
-                wd_raw[t // 2][:, t % 2, g * K_PASS : (g + 1) * K_PASS]
-                for g in range(first_pass, first_pass + 2)
-                for t in range(R_GROUPS)
-            ]
-            return transpose_weight(blocks, ident[:])
-
-        def quantise_wd(first_pass, grouped):
-            passes = slice(first_pass, first_pass + 2)
-            quantise(
-                grouped[:],
-                wd_codes[:, passes, :, :].rearrange("p g t q -> p (g t q)"),
-                wd_scales[:, passes, :, :].rearrange("p g t q -> p (g t q)"),
+        def quantise(unit):
+            pool = stage if unit[0] == TOKEN else keep
+            name = "x" if unit[0] == TOKEN else "%s%d%d" % unit
+            unit_codes = pool.tile([P, 4, P], U32, name="codes_" + name, align_bytes=64)
+            unit_scales = pool.tile([P, 4, P], U8, name="scales_" + name, align_bytes=64)
+            nc.vector.quantize_mx(
+                out=unit_codes[:].rearrange("p b r -> p (b r)").bitcast(FP8X4),
+                scales=unit_scales[:].rearrange("p b r -> p (b r)"),
+                in_=grouped[unit][:],
             )
+            codes[unit], scales[unit] = unit_codes, unit_scales
 
-        wu_mx = {}
+        lat_banks, lat_grouped, lat_codes, lat_scales = {}, {}, {}, {}
 
-        def transpose_wu(kind, half):
-            blocks = [wu_raw[(kind, half)][:, n, :] for n in range(BLOCKS_PER_CHUNK)]
-            matrix = split_pairs[:].rearrange("p e j -> p (e j)") if kind == KEYS else ident[:]
-            return transpose_weight(blocks, matrix)
-
-        def quantise_wu(kind, half, grouped):
-            columns = BLOCKS_PER_CHUNK * P
-            wu_codes = keep.tile([P, columns], U32, name="wu_codes%d%d" % (kind, half), align_bytes=64)
-            wu_scales = keep.tile([P, columns], U8, name="wu_scales%d%d" % (kind, half), align_bytes=64)
-            quantise(grouped[:], wu_codes[:], wu_scales[:])
-            wu_mx[(kind, half)] = (wu_codes, wu_scales)
-
-        x_grouped, x_mx, lat_banks, lat_grouped, lat_mx = {}, {}, {}, {}, {}
-
-        def stage_transpose_x(n):
-            x_grouped[n] = token_stage.tile(
-                [P, C_PASSES * K_PASS], BF16, name="x_grouped", tag="x_grouped", align_bytes=64
-            )
-            blocks = [x_raw[n // 2][:, n % 2, g * K_PASS : (g + 1) * K_PASS] for g in range(C_PASSES)]
-            transpose_blocks(nc, psum, x_grouped[n][:], ident[:], blocks)
-
-        def stage_quantise_x(n):
-            x_codes = token_stage.tile([P, C_PASSES, P], U32, tag="x_codes", align_bytes=64)
-            x_scales = token_stage.tile([P, C_PASSES, P], U8, tag="x_scales", align_bytes=64)
-            quantise(
-                x_grouped[n][:],
-                x_codes[:].rearrange("p g r -> p (g r)"),
-                x_scales[:].rearrange("p g r -> p (g r)"),
-            )
-            x_mx[n] = (x_codes, x_scales)
-
-        def stage_latent(n):
-            x_codes, x_scales = x_mx[n]
+        def latent(n):
+            x_codes, x_scales = codes[(TOKEN, n, 0)], scales[(TOKEN, n, 0)]
             lat_bank = psum.tile([P, R_GROUPS, P], F32, tag="bank")
             for t in range(R_GROUPS):
                 for g in range(C_PASSES):
                     nc.tensor.matmul_mx(
                         out=lat_bank[:, t, :],
-                        lhsT=wd_codes[:, g, t, :].bitcast(FP8X4),
-                        lhsT_scale=wd_scales[:, g, t, :],
+                        lhsT=codes[(DOWN, t, 0)][:, g, :].bitcast(FP8X4),
+                        lhsT_scale=scales[(DOWN, t, 0)][:, g, :],
                         rhs=x_codes[:, g, :].bitcast(FP8X4),
                         rhs_scale=x_scales[:, g, :],
                         start=(g == 0),
@@ -202,88 +179,70 @@ def tile_mla_pa_kernel(
                     )
             lat_banks[n] = lat_bank
 
-        def stage_round_latent(n):
-            lat_grouped[n] = token_stage.tile(
-                [P, P, R_GROUPS], BF16, name="lat_grouped", tag="lat_grouped", align_bytes=64
+        def round_latent(n, engine):
+            tile = stage.tile([P, P, R_GROUPS], BF16, name="lat_grouped", tag="lat_grouped", align_bytes=64)
+            copy_out = nc.vector.tensor_copy if engine == "v" else nc.scalar.copy
+            copy_out(out=tile[:], in_=lat_banks[n][:].rearrange("p t r -> p r t"))
+            lat_grouped[n] = tile
+
+        def quantise_latent(n):
+            c_tile = stage.tile([P, P], U32, name="lat_codes", tag="lat_codes", align_bytes=64, bufs=4)
+            s_tile = stage.tile([P, P], U8, name="lat_scales", tag="lat_scales", align_bytes=64, bufs=4)
+            nc.vector.quantize_mx(
+                out=c_tile[:].bitcast(FP8X4),
+                scales=s_tile[:],
+                in_=lat_grouped[n][:].rearrange("p r t -> p (r t)"),
             )
-            nc.vector.tensor_copy(out=lat_grouped[n][:], in_=lat_banks[n][:].rearrange("p t r -> p r t"))
+            lat_codes[n], lat_scales[n] = c_tile, s_tile
 
-        def stage_quantise_latent(n):
-            lat_codes = token_stage.tile([P, P], U32, tag="lat_codes", align_bytes=64)
-            lat_scales = token_stage.tile([P, P], U8, tag="lat_scales", align_bytes=64)
-            quantise(lat_grouped[n][:].rearrange("p r t -> p (r t)"), lat_codes[:], lat_scales[:])
-            lat_mx[n] = (lat_codes, lat_scales)
+        order = []
+        for pair in range(4):
+            for chunk in range(CHUNKS):
+                for i in (2 * pair, 2 * pair + 1):
+                    order.append((i, chunk))
 
-        wd_first = transpose_wd(0)
-        wd_second = transpose_wd(2)
-        quantise_wd(0, wd_first)
-        stage_transpose_x(0)
-        stage_transpose_x(1)
-        quantise_wd(2, wd_second)
-        keys_low = transpose_wu(KEYS, 0)
-        stage_quantise_x(0)
-        stage_quantise_x(1)
-        values_low = transpose_wu(VALUES, 0)
-        quantise_wu(KEYS, 0, keys_low)
-        stage_latent(0)
-        stage_latent(1)
-        quantise_wu(VALUES, 0, values_low)
-        stage_round_latent(0)
-        stage_round_latent(1)
-        stage_quantise_latent(0)
-        keys_high = transpose_wu(KEYS, 1)
-        values_high = transpose_wu(VALUES, 1)
-        quantise_wu(KEYS, 1, keys_high)
-        quantise_wu(VALUES, 1, values_high)
-
-        def project(bank, n, kind, step):
-            lat_codes, lat_scales = lat_mx[n]
-            wu_codes, wu_scales = wu_mx[(kind, step // BANKS_PER_CHUNK)]
-            columns = slice((step % BANKS_PER_CHUNK) * BANK, (step % BANKS_PER_CHUNK + 1) * BANK)
+        def project(bank, n, kind, chunk):
+            unit = (UP, kind, chunk)
             nc.tensor.matmul_mx(
                 out=bank,
-                lhsT=lat_codes[:].bitcast(FP8X4),
-                lhsT_scale=lat_scales[:],
-                rhs=wu_codes[:, columns].bitcast(FP8X4),
-                rhs_scale=wu_scales[:, columns],
+                lhsT=lat_codes[n][:].bitcast(FP8X4),
+                lhsT_scale=lat_scales[n][:],
+                rhs=codes[unit][:].rearrange("p b r -> p (b r)").bitcast(FP8X4),
+                rhs_scale=scales[unit][:].rearrange("p b r -> p (b r)"),
                 start=True,
                 stop=True,
             )
 
-        def store_two_banks(out_view, i, step, result):
-            columns = slice((step - 1) * BANK, (step + 1) * BANK)
-            nc.sync.dma_start(out=out_view[:, i, columns], in_=result[:, columns])
+        k_tiles, v_tiles = {}, {}
 
-        def add_products(i, step, products, k_rot):
-            heads = slice(step * HEADS_PER_BANK, (step + 1) * HEADS_PER_BANK)
-            nc.gpsimd.tensor_tensor(
-                out=k_rot[:, heads, :], in0=products[:, :, 0, :], in1=products[:, :, 1, :], op=ALU.add
+        def copy_values(i, chunk, v_bank, engine):
+            half = (chunk % 2) * BANK
+            copy_out = nc.vector.tensor_copy if engine == "v" else nc.scalar.copy
+            copy_out(
+                out=v_tiles[i][:, half : half + BANK], in_=v_bank[:]
             )
-            if step % 2 == 1:
-                store_two_banks(k_out_view, i, step, k_rot[:].rearrange("p h d -> p (h d)"))
 
-        def project_step(i, step, k_rot, v_sb):
+        def step(i, chunk, values_engine, after_products, after_step):
+            if chunk % 2 == 0:
+                k_tiles[i] = results.tile([P, 2 * HEADS_PER_BANK, D], F32, name="k_rot", tag="k_rot")
+                v_tiles[i] = results.tile([P, 2 * BANK], F32, name="v_sb", tag="v_sb")
             k_bank = psum.tile([P, HEADS_PER_BANK, D], F32, tag="bank")
-            project(k_bank[:].rearrange("p h d -> p (h d)"), i, KEYS, step)
+            project(k_bank[:].rearrange("p h d -> p (h d)"), i, KEYS, chunk)
             v_bank = psum.tile([P, BANK], F32, tag="bank")
-            project(v_bank[:], i, VALUES, step)
+            project(v_bank[:], i, VALUES, chunk)
 
             squares = stats.tile([P, HEADS_PER_BANK, D], BF16, tag="squares", bufs=2)
             sumsq = stats.tile([P, HEADS_PER_BANK], F32, tag="sumsq")
             rstd = stats.tile([P, HEADS_PER_BANK], F32, tag="rstd")
             for h in range(HEADS_PER_BANK):
                 nc.scalar.activation(
-                    out=squares[:, h, :],
-                    in_=k_bank[:, h, :],
-                    func=ACT.Square,
-                    accum_out=sumsq[:, h : h + 1],
+                    out=squares[:, h, :], in_=k_bank[:, h, :], func=ACT.Square, accum_out=sumsq[:, h : h + 1]
                 )
-            if step != VECTOR_VALUES_STEP:
-                nc.scalar.copy(out=v_sb[:, step * BANK : (step + 1) * BANK], in_=v_bank[:])
+            if values_engine == "s":
+                copy_values(i, chunk, v_bank, "s")
             nc.scalar.activation(
                 out=rstd[:], in_=sumsq[:], func=ACT.Abs_reciprocal_sqrt, scale=1.0 / D, bias=EPS
             )
-
             products = results.tile([P, HEADS_PER_BANK, 2, D], F32, tag="products", bufs=4)
             for h in range(HEADS_PER_BANK):
                 nc.vector.scalar_tensor_tensor(
@@ -294,24 +253,68 @@ def tile_mla_pa_kernel(
                     op0=ALU.mult,
                     op1=ALU.mult,
                 )
-            add_products(i, step, products, k_rot)
-            if step == VECTOR_VALUES_STEP:
-                nc.vector.tensor_copy(out=v_sb[:, step * BANK : (step + 1) * BANK], in_=v_bank[:])
-            if step % 2 == 1:
-                store_two_banks(v_out_view, i, step, v_sb[:])
+            after_products()
+            heads = slice((chunk % 2) * HEADS_PER_BANK, (chunk % 2 + 1) * HEADS_PER_BANK)
+            last = (i, chunk) == order[-1]
+            add_engine = nc.vector if last else nc.gpsimd
+            add_engine.tensor_tensor(
+                out=k_tiles[i][:, heads, :], in0=products[:, :, 0, :], in1=products[:, :, 1, :], op=ALU.add
+            )
+            if values_engine == "v":
+                copy_values(i, chunk, v_bank, "v")
+            if i >= TOKEN_TILES - 2 and chunk >= 2:
+                columns = slice(chunk * BANK, (chunk + 1) * BANK)
+                nc.sync.dma_start(out=v_out_view[:, i, columns], in_=v_tiles[i][:, (chunk % 2) * BANK : (chunk % 2 + 1) * BANK])
+                nc.sync.dma_start(
+                    out=k_out_view[:, i, columns], in_=k_tiles[i][:, heads, :].rearrange("p h d -> p (h d)")
+                )
+            elif chunk % 2 == 1:
+                columns = slice((chunk - 1) * BANK, (chunk + 1) * BANK)
+                nc.sync.dma_start(out=v_out_view[:, i, columns], in_=v_tiles[i][:])
+                nc.sync.dma_start(
+                    out=k_out_view[:, i, columns], in_=k_tiles[i][:].rearrange("p h d -> p (h d)")
+                )
+            after_step()
 
-        for i in range(TOKEN_TILES):
-            k_rot = results.tile([P, HEADS, D], F32, tag="k_rot")
-            v_sb = results.tile([P, HEADS * D], F32, tag="v_sb")
-            project_step(i, 0, k_rot, v_sb)
-            if i + 2 < TOKEN_TILES:
-                stage_transpose_x(i + 2)
-                stage_quantise_x(i + 2)
-            if i + 1 < TOKEN_TILES:
-                stage_quantise_latent(i + 1)
-            project_step(i, 1, k_rot, v_sb)
-            project_step(i, 2, k_rot, v_sb)
-            project_step(i, 3, k_rot, v_sb)
-            if i + 2 < TOKEN_TILES:
-                stage_latent(i + 2)
-                stage_round_latent(i + 2)
+        actions = {}
+
+        def at(s, phase, action):
+            actions.setdefault((s, phase), []).append(action)
+
+        def plan_quantise(unit, s):
+            at(s, "products", lambda: quantise(unit))
+
+        def plan_unit(unit, s):
+            at(s, "step", lambda: transpose(unit, "sv"))
+            plan_quantise(unit, s + 1)
+            if unit[0] == TOKEN:
+                n = unit[1]
+                at(s + 4, "step", lambda: latent(n))
+                at(s + 4, "step", lambda: round_latent(n, "s"))
+                at(s + 5, "products", lambda: quantise_latent(n))
+
+        for n, unit in enumerate(prologue):
+            if n > 0:
+                quantise(prologue[n - 1])
+            if n in (8, 9):
+                quantise_latent(n - 8)
+            transpose(unit, "sv" if n % 2 else "ss")
+            if n == 4:
+                spread_gain()
+                make_rope_table(slice(0, 4))
+                make_rope_table(slice(4, TOKEN_TILES))
+            if n in (6, 7):
+                latent(n - 6)
+                round_latent(n - 6, "v")
+        plan_quantise(prologue[-1], 0)
+        for unit, s in planned:
+            plan_unit(unit, s)
+
+        for s, (i, chunk) in enumerate(order):
+            step(
+                i,
+                chunk,
+                "v" if s > 20 and s % 4 == 2 else "s",
+                lambda: [action() for action in actions.get((s, "products"), [])],
+                lambda: [action() for action in actions.get((s, "step"), [])],
+            )

@@ -70,9 +70,8 @@ def tile_mla_pa_kernel(
         down = [(DOWN, t, 0) for t in range(R_GROUPS)]
         token = [(TOKEN, n, 0) for n in range(TOKEN_TILES)]
         up = [[(UP, kind, chunk) for kind in (KEYS, VALUES)] for chunk in range(CHUNKS)]
-        prologue = [token[0]] + down + [token[1]] + up[0] + up[1]
-        planned = [(up[2][0], 0), (token[2], 0), (up[2][1], 1), (token[3], 1), (up[3][0], 3), (up[3][1], 4)]
-        planned += [(token[4], 7), (token[5], 8), (token[6], 12), (token[7], 13)]
+        units = [token[0]] + down + up[0] + [token[1]] + up[1] + up[2] + [token[2]] + up[3] + token[3:]
+        prologue, behind_step = units[:14], units[14:]
         gain_row = keep.tile([P, D], BF16, name="gain_row")
         nc.vector.memset(gain_row[:], 0.0)
         ones = keep.tile([P, P], BF16, name="ones")
@@ -83,7 +82,7 @@ def tile_mla_pa_kernel(
 
         cos_bf = keep.tile([P, TOKEN_TILES, HALF], BF16, name="cos_bf")
         sin_bf = keep.tile([P, TOKEN_TILES, HALF], BF16, name="sin_bf")
-        for n, unit in enumerate(prologue + [unit for unit, s in planned]):
+        for n, unit in enumerate(units):
             load(unit)
             if n == 4:
                 nc.sync.dma_start(out=cos_bf[:], in_=freqs_cos.rearrange("(p i) j -> p i j", i=TOKEN_TILES))
@@ -281,40 +280,33 @@ def tile_mla_pa_kernel(
         def at(s, phase, action):
             actions.setdefault((s, phase), []).append(action)
 
-        def plan_quantise(unit, s):
-            at(s, "products", lambda: quantise(unit))
-
-        def plan_unit(unit, s):
-            at(s, "step", lambda: transpose(unit, "sv"))
-            plan_quantise(unit, s + 1)
-            if unit[0] == TOKEN:
-                n = unit[1]
-                at(s + 4, "step", lambda: latent(n))
-                at(s + 4, "step", lambda: round_latent(n, "s"))
-                at(s + 5, "products", lambda: quantise_latent(n))
-
         for n, unit in enumerate(prologue):
+            if n in (9, 11):
+                quantise_latent((n - 9) // 2)
             if n > 0:
                 quantise(prologue[n - 1])
-            if n in (8, 9):
-                quantise_latent(n - 8)
             transpose(unit, "sv" if n % 2 else "ss")
             if n == 4:
                 spread_gain()
                 make_rope_table(slice(0, 4))
                 make_rope_table(slice(4, TOKEN_TILES))
-            if n in (6, 7):
-                latent(n - 6)
-                round_latent(n - 6, "v")
-        plan_quantise(prologue[-1], 0)
-        for unit, s in planned:
-            plan_unit(unit, s)
+            if n in (7, 9):
+                latent((n - 7) // 2)
+                round_latent((n - 7) // 2, "v")
+        at(0, "products", lambda: quantise(prologue[-1]))
+        for s, unit in enumerate(behind_step):
+            at(s, "step", lambda unit=unit: transpose(unit, "sv"))
+            at(s + 1, "products", lambda unit=unit: quantise(unit))
+        for n in range(2, TOKEN_TILES):
+            at(2 * n - 2, "step", lambda n=n: latent(n))
+            at(2 * n - 2, "step", lambda n=n: round_latent(n, "s"))
+            at(2 * n - 1, "products", lambda n=n: quantise_latent(n))
 
         for s, (i, chunk) in enumerate(order):
             step(
                 i,
                 chunk,
-                "v" if s > 20 and s % 4 == 2 else "s",
+                "v" if s >= 12 and s % 5 == 2 else "s",
                 lambda: [action() for action in actions.get((s, "products"), [])],
                 lambda: [action() for action in actions.get((s, "step"), [])],
             )

@@ -71,7 +71,7 @@ def tile_mla_pa_kernel(
         token = [(TOKEN, n, 0) for n in range(TOKEN_TILES)]
         up = [[(UP, kind, chunk) for kind in (KEYS, VALUES)] for chunk in range(CHUNKS)]
         units = [token[0]] + down + up[0] + [token[1]] + up[1] + up[2] + [token[2]] + up[3] + token[3:]
-        prologue, behind_step = units[:14], units[14:]
+        prologue = units[:13]
         gain_row = keep.tile([P, D], BF16, name="gain_row")
         nc.vector.memset(gain_row[:], 0.0)
         ones = keep.tile([P, P], BF16, name="ones")
@@ -195,10 +195,13 @@ def tile_mla_pa_kernel(
             lat_codes[n], lat_scales[n] = c_tile, s_tile
 
         order = []
-        for pair in range(4):
+        for pair in range(2):
             for chunk in range(CHUNKS):
                 for i in (2 * pair, 2 * pair + 1):
                     order.append((i, chunk))
+        for i in range(4, TOKEN_TILES):
+            for chunk in range(CHUNKS):
+                order.append((i, chunk))
 
         def project(bank, n, kind, chunk):
             unit = (UP, kind, chunk)
@@ -212,7 +215,7 @@ def tile_mla_pa_kernel(
                 stop=True,
             )
 
-        k_tiles, v_tiles = {}, {}
+        k_tiles, v_tiles, k_stores = {}, {}, []
 
         def copy_values(i, chunk, v_bank, engine):
             half = (chunk % 2) * BANK
@@ -261,18 +264,24 @@ def tile_mla_pa_kernel(
             )
             if values_engine == "v":
                 copy_values(i, chunk, v_bank, "v")
-            if i >= TOKEN_TILES - 2 and chunk >= 2:
-                columns = slice(chunk * BANK, (chunk + 1) * BANK)
-                nc.sync.dma_start(out=v_out_view[:, i, columns], in_=v_tiles[i][:, (chunk % 2) * BANK : (chunk % 2 + 1) * BANK])
-                nc.sync.dma_start(
-                    out=k_out_view[:, i, columns], in_=k_tiles[i][:, heads, :].rearrange("p h d -> p (h d)")
-                )
-            elif chunk % 2 == 1:
-                columns = slice((chunk - 1) * BANK, (chunk + 1) * BANK)
-                nc.sync.dma_start(out=v_out_view[:, i, columns], in_=v_tiles[i][:])
-                nc.sync.dma_start(
-                    out=k_out_view[:, i, columns], in_=k_tiles[i][:].rearrange("p h d -> p (h d)")
-                )
+            single = i == TOKEN_TILES - 1 and chunk >= 2
+            if single or chunk % 2 == 1:
+                if single:
+                    columns = slice(chunk * BANK, (chunk + 1) * BANK)
+                    part = slice((chunk % 2) * BANK, (chunk % 2 + 1) * BANK)
+                else:
+                    columns = slice((chunk - 1) * BANK, (chunk + 1) * BANK)
+                    part = slice(0, 2 * BANK)
+                nc.sync.dma_start(out=v_out_view[:, i, columns], in_=v_tiles[i][:, part])
+            if k_stores:
+                out, rows = k_stores.pop(0)
+                nc.sync.dma_start(out=out, in_=rows)
+            if single or chunk % 2 == 1:
+                k_rows = k_tiles[i][:].rearrange("p h d -> p (h d)")
+                k_stores.append((k_out_view[:, i, columns], k_rows[:, part]))
+            if last:
+                out, rows = k_stores.pop(0)
+                nc.sync.dma_start(out=out, in_=rows)
             after_step()
 
         actions = {}
@@ -281,8 +290,8 @@ def tile_mla_pa_kernel(
             actions.setdefault((s, phase), []).append(action)
 
         for n, unit in enumerate(prologue):
-            if n in (9, 11):
-                quantise_latent((n - 9) // 2)
+            if n in (10, 12):
+                quantise_latent((n - 10) // 2)
             if n > 0:
                 quantise(prologue[n - 1])
             transpose(unit, "sv" if n % 2 else "ss")
@@ -290,23 +299,34 @@ def tile_mla_pa_kernel(
                 spread_gain()
                 make_rope_table(slice(0, 4))
                 make_rope_table(slice(4, TOKEN_TILES))
-            if n in (7, 9):
-                latent((n - 7) // 2)
-                round_latent((n - 7) // 2, "v")
+            if n in (8, 10):
+                latent((n - 8) // 2)
+                round_latent((n - 8) // 2, "v")
         at(0, "products", lambda: quantise(prologue[-1]))
-        for s, unit in enumerate(behind_step):
-            at(s, "step", lambda unit=unit: transpose(unit, "sv"))
-            at(s + 1, "products", lambda unit=unit: quantise(unit))
-        for n in range(2, TOKEN_TILES):
-            at(2 * n - 2, "step", lambda n=n: latent(n))
-            at(2 * n - 2, "step", lambda n=n: round_latent(n, "s"))
-            at(2 * n - 1, "products", lambda n=n: quantise_latent(n))
+
+        def plan_unit(unit, s):
+            at(s, "step", lambda: transpose(unit, "sv"))
+            at(s + 1, "products", lambda: quantise(unit))
+
+        def plan_latent(n, s):
+            at(s, "step", lambda: latent(n))
+            at(s, "step", lambda: round_latent(n, "s"))
+            at(s + 1, "products", lambda: quantise_latent(n))
+
+        plan_unit(up[3][0], 0)
+        plan_unit(up[3][1], 0)
+        plan_unit(token[3], 1)
+        plan_latent(2, 3)
+        plan_latent(3, 5)
+        for n in range(4, TOKEN_TILES):
+            plan_unit(token[n], 4 * n - 10)
+            plan_latent(n, 4 * n - 5)
 
         for s, (i, chunk) in enumerate(order):
             step(
                 i,
                 chunk,
-                "v" if s >= 12 and s % 5 == 2 else "s",
+                "v" if s >= 12 and s % 6 == 2 else "s",
                 lambda: [action() for action in actions.get((s, "products"), [])],
                 lambda: [action() for action in actions.get((s, "step"), [])],
             )

@@ -80,42 +80,33 @@ def tile_mla_pa_kernel(
         nc.vector.memset(one[:], 1.0)
         nc.scalar.activation(out=one[:], in_=one[:], func=ACT.Abs_reciprocal_sqrt)
 
-        cos_bf = keep.tile([P, TOKEN_TILES, HALF], BF16, name="cos_bf")
-        sin_bf = keep.tile([P, TOKEN_TILES, HALF], BF16, name="sin_bf")
+        angles = keep.tile([P, 3, TOKEN_TILES, HALF], BF16, name="angles")
         for n, unit in enumerate(units):
             load(unit)
-            if n == 4:
-                nc.sync.dma_start(out=cos_bf[:], in_=freqs_cos.rearrange("(p i) j -> p i j", i=TOKEN_TILES))
-                nc.sync.dma_start(out=sin_bf[:], in_=freqs_sin.rearrange("(p i) j -> p i j", i=TOKEN_TILES))
+            if n == 0:
+                nc.sync.dma_start(out=angles[:, 1], in_=freqs_cos.rearrange("(p i) j -> p i j", i=TOKEN_TILES))
+                nc.sync.dma_start(out=angles[:, 2], in_=freqs_sin.rearrange("(p i) j -> p i j", i=TOKEN_TILES))
                 nc.sync.dma_start(out=gain_row[0:1, :], in_=k_norm_w.unsqueeze(0))
 
         ident = keep.tile([P, P], F32, name="ident")
         make_identity(nc, ident[:])
 
         rope_table = keep.tile([P, TOKEN_TILES, 2, HALF, 2], F32, name="rope_table")
-        gain = keep.tile([P, HALF, 2], F32, name="gain")
-        neg_gain = keep.tile([P, HALF, 2], F32, name="neg_gain")
 
-        def spread_gain():
+        def make_rope_table():
             bank = psum.tile([P, BANK], F32, tag="bank")
             nc.tensor.matmul(bank[:, 0:D], lhsT=ones[:], rhs=gain_row[:], start=True, stop=True)
-            nc.scalar.copy(out=gain[:].rearrange("p j e -> p (j e)"), in_=bank[:, 0:D])
-            nc.gpsimd.tensor_scalar(
-                out=neg_gain[:], in0=gain[:], scalar1=-1.0, scalar2=0.0, op0=ALU.mult, op1=ALU.add
+            gain = keep.tile([P, 2, HALF, 2], F32, name="gain")
+            nc.scalar.copy(
+                out=gain[:],
+                in_=bank[:, 0:D].rearrange("p (j e) -> p e j", e=2).unsqueeze(3).to_broadcast([P, 2, HALF, 2]),
             )
-
-        def make_rope_table(tiles):
-            count = tiles.stop - tiles.start
-            for e, w, angle, factor in [
-                (0, 0, cos_bf, gain),
-                (0, 1, sin_bf, gain),
-                (1, 0, sin_bf, neg_gain),
-                (1, 1, cos_bf, gain),
-            ]:
-                nc.gpsimd.tensor_tensor(
-                    out=rope_table[:, tiles, e, :, w],
-                    in0=angle[:, tiles, :],
-                    in1=factor[:, :, e].unsqueeze(1).to_broadcast([P, count, HALF]),
+            nc.vector.tensor_scalar(out=angles[:, 0], in0=angles[:, 2], scalar1=-1.0, scalar2=None, op0=ALU.mult)
+            for e in range(2):
+                nc.vector.tensor_tensor(
+                    out=rope_table[:, :, e, :, :],
+                    in0=angles[:, 1 - e : 3 - e].rearrange("p w i j -> p i j w"),
+                    in1=gain[:, e].unsqueeze(1).to_broadcast([P, TOKEN_TILES, HALF, 2]),
                     op=ALU.mult,
                 )
 
@@ -233,6 +224,20 @@ def tile_mla_pa_kernel(
             v_bank = psum.tile([P, BANK], F32, tag="bank")
             project(v_bank[:], i, VALUES, chunk)
 
+            last = (i, chunk) == order[-1]
+            single = i == TOKEN_TILES - 1 and chunk >= 2
+            stored = single or chunk % 2 == 1
+            first = chunk if single else chunk - 1
+            columns = slice(first * BANK, (chunk + 1) * BANK)
+            part = slice((first % 2) * BANK, (chunk % 2 + 1) * BANK)
+
+            def store_behind_values():
+                if stored:
+                    nc.sync.dma_start(out=v_out_view[:, i, columns], in_=v_tiles[i][:, part])
+                if k_stores:
+                    out, rows = k_stores.pop(0)
+                    nc.sync.dma_start(out=out, in_=rows)
+
             squares = stats.tile([P, HEADS_PER_BANK, D], BF16, tag="squares", bufs=2)
             sumsq = stats.tile([P, HEADS_PER_BANK], F32, tag="sumsq")
             rstd = stats.tile([P, HEADS_PER_BANK], F32, tag="rstd")
@@ -242,10 +247,29 @@ def tile_mla_pa_kernel(
                 )
             if values_engine == "s":
                 copy_values(i, chunk, v_bank, "s")
+                store_behind_values()
             nc.scalar.activation(
                 out=rstd[:], in_=sumsq[:], func=ACT.Abs_reciprocal_sqrt, scale=1.0 / D, bias=EPS
             )
             products = results.tile([P, HEADS_PER_BANK, 2, D], F32, tag="products", bufs=4)
+            first_head = (chunk % 2) * HEADS_PER_BANK
+
+            def add_products(engine, start, stop):
+                engine.tensor_tensor(
+                    out=k_tiles[i][:, first_head + start : first_head + stop, :],
+                    in0=products[:, start:stop, 0, :],
+                    in1=products[:, start:stop, 1, :],
+                    op=ALU.add,
+                )
+
+            def add_and_store(start, stop):
+                add_products(nc.vector, start, stop)
+                rows = k_tiles[i][:, first_head + start : first_head + stop, :]
+                nc.sync.dma_start(
+                    out=k_out_view[:, i, chunk * BANK + start * D : chunk * BANK + stop * D],
+                    in_=rows.rearrange("p h d -> p (h d)"),
+                )
+
             for h in range(HEADS_PER_BANK):
                 nc.vector.scalar_tensor_tensor(
                     out=products[:, h, :, :].rearrange("p e (j w) -> p (e j) w", w=2),
@@ -255,33 +279,19 @@ def tile_mla_pa_kernel(
                     op0=ALU.mult,
                     op1=ALU.mult,
                 )
+                if last and h == 2:
+                    add_and_store(0, 2)
             after_products()
-            heads = slice((chunk % 2) * HEADS_PER_BANK, (chunk % 2 + 1) * HEADS_PER_BANK)
-            last = (i, chunk) == order[-1]
-            add_engine = nc.vector if last else nc.gpsimd
-            add_engine.tensor_tensor(
-                out=k_tiles[i][:, heads, :], in0=products[:, :, 0, :], in1=products[:, :, 1, :], op=ALU.add
-            )
-            if values_engine == "v":
-                copy_values(i, chunk, v_bank, "v")
-            single = i == TOKEN_TILES - 1 and chunk >= 2
-            if single or chunk % 2 == 1:
-                if single:
-                    columns = slice(chunk * BANK, (chunk + 1) * BANK)
-                    part = slice((chunk % 2) * BANK, (chunk % 2 + 1) * BANK)
-                else:
-                    columns = slice((chunk - 1) * BANK, (chunk + 1) * BANK)
-                    part = slice(0, 2 * BANK)
-                nc.sync.dma_start(out=v_out_view[:, i, columns], in_=v_tiles[i][:, part])
-            if k_stores:
-                out, rows = k_stores.pop(0)
-                nc.sync.dma_start(out=out, in_=rows)
-            if single or chunk % 2 == 1:
+            if last:
+                add_and_store(2, HEADS_PER_BANK)
+            else:
+                add_products(nc.gpsimd, 0, HEADS_PER_BANK)
+            if stored and not last:
                 k_rows = k_tiles[i][:].rearrange("p h d -> p (h d)")
                 k_stores.append((k_out_view[:, i, columns], k_rows[:, part]))
-            if last:
-                out, rows = k_stores.pop(0)
-                nc.sync.dma_start(out=out, in_=rows)
+            if values_engine == "v":
+                copy_values(i, chunk, v_bank, "v")
+                store_behind_values()
             after_step()
 
         actions = {}
@@ -295,10 +305,8 @@ def tile_mla_pa_kernel(
             if n > 0:
                 quantise(prologue[n - 1])
             transpose(unit, "sv" if n % 2 else "ss")
-            if n == 4:
-                spread_gain()
-                make_rope_table(slice(0, 4))
-                make_rope_table(slice(4, TOKEN_TILES))
+            if n == 0:
+                make_rope_table()
             if n in (8, 10):
                 latent((n - 8) // 2)
                 round_latent((n - 8) // 2, "v")

@@ -312,8 +312,8 @@ def tile_mla_pa_kernel(
                 round_latent((n - 8) // 2, "v")
         at(0, "products", lambda: quantise(prologue[-1]))
 
-        def plan_unit(unit, s):
-            at(s, "step", lambda: transpose(unit, "sv"))
+        def plan_unit(unit, s, engines):
+            at(s, "step", lambda: transpose(unit, engines))
             at(s + 1, "products", lambda: quantise(unit))
 
         def plan_latent(n, s):
@@ -321,20 +321,20 @@ def tile_mla_pa_kernel(
             at(s, "step", lambda: round_latent(n, "s"))
             at(s + 1, "products", lambda: quantise_latent(n))
 
-        plan_unit(up[3][0], 0)
-        plan_unit(up[3][1], 0)
-        plan_unit(token[3], 1)
+        plan_unit(up[3][0], 0, "ss")
+        plan_unit(up[3][1], 0, "ss")
+        plan_unit(token[3], 1, "ss")
         plan_latent(2, 3)
         plan_latent(3, 5)
         for n in range(4, TOKEN_TILES):
-            plan_unit(token[n], 4 * n - 10)
+            plan_unit(token[n], 4 * n - 10, "sv")
             plan_latent(n, 4 * n - 5)
 
         for s, (i, chunk) in enumerate(order):
             step(
                 i,
                 chunk,
-                "v" if s >= 12 and s % 6 == 2 else "s",
+                "s",
                 lambda: [action() for action in actions.get((s, "products"), [])],
                 lambda: [action() for action in actions.get((s, "step"), [])],
             )

@@ -206,7 +206,9 @@ def tile_mla_pa_kernel(
                 stop=True,
             )
 
-        k_tiles, v_tiles, k_stores = {}, {}, []
+        k_tiles, v_tiles, k_stores, pair_products = {}, {}, [], [None]
+        all_sumsq = keep.tile([P, len(order), HEADS_PER_BANK], F32, name="all_sumsq")
+        all_rstd = keep.tile([P, len(order), HEADS_PER_BANK], F32, name="all_rstd")
 
         def copy_values(i, chunk, v_bank, engine):
             half = (chunk % 2) * BANK
@@ -239,8 +241,8 @@ def tile_mla_pa_kernel(
                     nc.sync.dma_start(out=out, in_=rows)
 
             squares = stats.tile([P, HEADS_PER_BANK, D], BF16, tag="squares", bufs=2)
-            sumsq = stats.tile([P, HEADS_PER_BANK], F32, tag="sumsq")
-            rstd = stats.tile([P, HEADS_PER_BANK], F32, tag="rstd")
+            s = order.index((i, chunk))
+            sumsq, rstd = all_sumsq[:, s, :], all_rstd[:, s, :]
             for h in range(HEADS_PER_BANK):
                 nc.scalar.activation(
                     out=squares[:, h, :], in_=k_bank[:, h, :], func=ACT.Square, accum_out=sumsq[:, h : h + 1]
@@ -249,9 +251,13 @@ def tile_mla_pa_kernel(
                 copy_values(i, chunk, v_bank, "s")
                 store_behind_values()
             nc.scalar.activation(
-                out=rstd[:], in_=sumsq[:], func=ACT.Abs_reciprocal_sqrt, scale=1.0 / D, bias=EPS
+                out=rstd, in_=sumsq, func=ACT.Abs_reciprocal_sqrt, scale=1.0 / D, bias=EPS
             )
-            products = results.tile([P, HEADS_PER_BANK, 2, D], F32, tag="products", bufs=4)
+            if s % 2 == 0:
+                pair_products[0] = results.tile(
+                    [P, 2, HEADS_PER_BANK, 2, D], F32, name="pair_products", tag="products", bufs=3
+                )
+            products = pair_products[0][:, s % 2]
             first_head = (chunk % 2) * HEADS_PER_BANK
 
             def add_products(engine, start, stop):

@@ -226,7 +226,8 @@ def tile_mla_pa_kernel(
             v_bank = psum.tile([P, BANK], F32, tag="bank")
             project(v_bank[:], i, VALUES, chunk)
 
-            last = (i, chunk) == order[-1]
+            s = order.index((i, chunk))
+            last = s == len(order) - 1
             single = i == TOKEN_TILES - 1 and chunk >= 2
             stored = single or chunk % 2 == 1
             first = chunk if single else chunk - 1
@@ -236,12 +237,11 @@ def tile_mla_pa_kernel(
             def store_behind_values():
                 if stored:
                     nc.sync.dma_start(out=v_out_view[:, i, columns], in_=v_tiles[i][:, part])
-                if k_stores:
-                    out, rows = k_stores.pop(0)
+                while k_stores and (last or k_stores[0][0] <= s - 2):
+                    unused, out, rows = k_stores.pop(0)
                     nc.sync.dma_start(out=out, in_=rows)
 
             squares = stats.tile([P, HEADS_PER_BANK, D], BF16, tag="squares", bufs=2)
-            s = order.index((i, chunk))
             sumsq, rstd = all_sumsq[:, s, :], all_rstd[:, s, :]
             for h in range(HEADS_PER_BANK):
                 nc.scalar.activation(
@@ -294,7 +294,7 @@ def tile_mla_pa_kernel(
                 add_products(nc.gpsimd, 0, HEADS_PER_BANK)
             if stored and not last:
                 k_rows = k_tiles[i][:].rearrange("p h d -> p (h d)")
-                k_stores.append((k_out_view[:, i, columns], k_rows[:, part]))
+                k_stores.append((s, k_out_view[:, i, columns], k_rows[:, part]))
             if values_engine == "v":
                 copy_values(i, chunk, v_bank, "v")
                 store_behind_values()
@@ -310,7 +310,7 @@ def tile_mla_pa_kernel(
                 quantise_latent((n - 10) // 2)
             if n > 0:
                 quantise(prologue[n - 1])
-            transpose(unit, "sv" if n % 2 else "ss")
+            transpose(unit, "sv" if n % 2 == 0 else "ss")
             if n == 0:
                 make_rope_table()
             if n in (8, 10):
@@ -327,13 +327,13 @@ def tile_mla_pa_kernel(
             at(s, "step", lambda: round_latent(n, "s"))
             at(s + 1, "products", lambda: quantise_latent(n))
 
-        plan_unit(up[3][0], 0, "ss")
-        plan_unit(up[3][1], 0, "ss")
-        plan_unit(token[3], 1, "ss")
+        plan_unit(up[3][0], 0, "sv")
+        plan_unit(up[3][1], 1, "ss")
+        plan_unit(token[3], 2, "sv")
         plan_latent(2, 3)
         plan_latent(3, 5)
         for n in range(4, TOKEN_TILES):
-            plan_unit(token[n], 4 * n - 10, "sv")
+            plan_unit(token[n], 4 * n - 12, "sv")
             plan_latent(n, 4 * n - 5)
 
         for s, (i, chunk) in enumerate(order):

from contextlib import ExitStack

import concourse.mybir as mybir
from concourse.masks import make_identity

F32 = mybir.dt.float32
BF16 = mybir.dt.bfloat16
U32 = mybir.dt.uint32
U8 = mybir.dt.uint8
FP8X4 = mybir.dt.float8_e4m3fn_x4
ALU = mybir.AluOpType
ACT = mybir.ActivationFunctionType

P = 128
PACK = 4
K_PASS = P * PACK
BANK = 512

TOKENS, C, R, HEADS, D = 1024, 2048, 512, 16, 128
EPS = 1e-6
HALF = D // 2
TOKEN_TILES = TOKENS // P
C_PASSES = C // K_PASS
R_GROUPS = R // P
HEADS_PER_BANK = BANK // D
CHUNKS = HEADS // HEADS_PER_BANK
KEYS, VALUES = 0, 1

FLOPS = 2 * TOKENS * C * R + 2 * TOKENS * R * 2 * HEADS * D

DOWN, TOKEN, UP = "down", "token", "up"


def tile_mla_pa_kernel(
    tc, x, w_kv_down, w_kv_up, k_norm_w, freqs_cos, freqs_sin, out_0, out_1
):
    nc = tc.nc
    x_view = x.flatten_outer_dims().rearrange("(p i) c -> p i c", i=TOKEN_TILES)
    wd_view = w_kv_down.rearrange("(q t) c -> q t c", t=R_GROUPS)
    wu_view = w_kv_up.rearrange("(n g q e) r -> n q g e r", g=2, q=P, e=2)
    k_out_view = out_0.flatten_outer_dims().rearrange("(p i h) d -> p i (h d)", i=TOKEN_TILES, h=HEADS)
    v_out_view = out_1.flatten_outer_dims().rearrange("(p i h) d -> p i (h d)", i=TOKEN_TILES, h=HEADS)

    with ExitStack() as stack:
        stack.enter_context(tc.manual_schedule())
        keep = stack.enter_context(tc.tile_pool(name="keep", bufs=1))
        stage = stack.enter_context(tc.tile_pool(name="stage", bufs=3))
        stats = stack.enter_context(tc.tile_pool(name="stats", bufs=4))
        results = stack.enter_context(tc.tile_pool(name="results", bufs=8))
        psum = stack.enter_context(tc.psum_pool(name="psum", bufs=8))

        raw = {}

        def load(unit):
            kind, a, b = unit
            tile = stage.tile([P, C], BF16, name="raw", tag="raw", bufs=14)
            if kind == DOWN:
                nc.sync.dma_start(out=tile[:], in_=wd_view[:, a, :])
            elif kind == TOKEN and a == 0:
                for g in range(C_PASSES):
                    nc.sync.dma_start(out=tile[:, g * K_PASS : (g + 1) * K_PASS], in_=x_view[:, a, g * K_PASS : (g + 1) * K_PASS])
            elif kind == TOKEN:
                nc.sync.dma_start(out=tile[:], in_=x_view[:, a, :])
            else:
                nc.sync.dma_start(
                    out=tile[:].rearrange("p (g e r) -> p g e r", g=2, e=2), in_=wu_view[a * CHUNKS + b]
                )
            raw[unit] = tile

        down = [(DOWN, t, 0) for t in range(R_GROUPS)]
        token = [(TOKEN, n, 0) for n in range(TOKEN_TILES)]
        up = [[(UP, kind, chunk) for kind in (KEYS, VALUES)] for chunk in range(CHUNKS)]
        units = [token[0]] + down + up[0] + [token[1]] + up[1] + up[2] + [token[2]] + up[3] + token[3:]
        prologue = units[:13]
        gain_row = keep.tile([P, D], BF16, name="gain_row")
        nc.vector.memset(gain_row[:], 0.0)
        ones = keep.tile([P, P], BF16, name="ones")
        nc.vector.memset(ones[:], 1.0)
        one = keep.tile([P, 1], F32, name="one")
        nc.vector.memset(one[:], 1.0)
        nc.scalar.activation(out=one[:], in_=one[:], func=ACT.Abs_reciprocal_sqrt)

        angles = keep.tile([P, 3, TOKEN_TILES, HALF], BF16, name="angles")
        for n, unit in enumerate(units):
            load(unit)
            if n == 0:
                nc.sync.dma_start(out=angles[:, 1], in_=freqs_cos.rearrange("(p i) j -> p i j", i=TOKEN_TILES))
                nc.sync.dma_start(out=angles[:, 2], in_=freqs_sin.rearrange("(p i) j -> p i j", i=TOKEN_TILES))
                nc.sync.dma_start(out=gain_row[0:1, :], in_=k_norm_w.unsqueeze(0))

        ident = keep.tile([P, P], F32, name="ident")
        make_identity(nc, ident[:])

        rope_table = keep.tile([P, TOKEN_TILES, 2, HALF, 2], F32, name="rope_table")

        def make_rope_table():
            bank = psum.tile([P, BANK], F32, tag="bank")
            nc.tensor.matmul(bank[:, 0:D], lhsT=ones[:], rhs=gain_row[:], start=True, stop=True)
            gain = keep.tile([P, 2, HALF, 2], F32, name="gain")
            nc.scalar.copy(
                out=gain[:],
                in_=bank[:, 0:D].rearrange("p (j e) -> p e j", e=2).unsqueeze(3).to_broadcast([P, 2, HALF, 2]),
            )
            nc.vector.tensor_scalar(out=angles[:, 0], in0=angles[:, 2], scalar1=-1.0, scalar2=None, op0=ALU.mult)
            for e in range(2):
                nc.vector.tensor_tensor(
                    out=rope_table[:, :, e, :, :],
                    in0=angles[:, 1 - e : 3 - e].rearrange("p w i j -> p i j w"),
                    in1=gain[:, e].unsqueeze(1).to_broadcast([P, TOKEN_TILES, HALF, 2]),
                    op=ALU.mult,
                )

        grouped, codes, scales = {}, {}, {}

        def transpose(unit, engines):
            words = raw[unit][:].bitcast(F32).rearrange("p (b w) -> p b w", b=4)
            tile = stage.tile([P, 4 * P * PACK], BF16, name="grouped", tag="grouped", align_bytes=64, bufs=5)
            grouped_words = tile[:].bitcast(F32).rearrange("p (b r u) -> p b r u", b=4, u=2)
            for pair in range(2):
                bank = psum.tile([P, 2, 2, P], F32, tag="bank")
                for a in range(2):
                    for u in range(2):
                        nc.tensor.transpose(bank[:, a, u, :], words[:, 2 * pair + a, u::2], ident[:])
                copy_out = nc.vector.tensor_copy if engines[pair] == "v" else nc.scalar.copy
                words_out = grouped_words[:, 2 * pair : 2 * pair + 2, :, :]
                if unit[0] != UP:
                    copy_out(out=words_out, in_=bank[:].rearrange("p a u r -> p a r u"))
                elif unit[1] == VALUES:
                    copy_out(
                        out=words_out.rearrange("p a r u -> p (a r u)").rearrange("p (r a u) -> p r a u", a=2, u=2),
                        in_=bank[:].rearrange("p a u r -> p r a u"),
                    )
                else:
                    for head in range(2):
                        rows = slice(head * HALF, (head + 1) * HALF)
                        copy_out(
                            out=words_out[:, head, :, :].rearrange("p (a j) u -> p a j u", a=2),
                            in_=bank[:, :, :, rows].rearrange("p a u j -> p a j u"),
                        )
            grouped[unit] = tile

        def quantise(unit):
            pool = stage if unit[0] == TOKEN else keep
            name = "x" if unit[0] == TOKEN else "%s%d%d" % unit
            unit_codes = pool.tile([P, 4, P], U32, name="codes_" + name, align_bytes=64)
            unit_scales = pool.tile([P, 4, P], U8, name="scales_" + name, align_bytes=64)
            nc.vector.quantize_mx(
                out=unit_codes[:].rearrange("p b r -> p (b r)").bitcast(FP8X4),
                scales=unit_scales[:].rearrange("p b r -> p (b r)"),
                in_=grouped[unit][:],
            )
            codes[unit], scales[unit] = unit_codes, unit_scales

        lat_banks, lat_grouped, lat_codes, lat_scales = {}, {}, {}, {}

        def latent(n):
            x_codes, x_scales = codes[(TOKEN, n, 0)], scales[(TOKEN, n, 0)]
            lat_bank = psum.tile([P, R_GROUPS, P], F32, tag="bank")
            for t in range(R_GROUPS):
                for g in range(C_PASSES):
                    nc.tensor.matmul_mx(
                        out=lat_bank[:, t, :],
                        lhsT=codes[(DOWN, t, 0)][:, g, :].bitcast(FP8X4),
                        lhsT_scale=scales[(DOWN, t, 0)][:, g, :],
                        rhs=x_codes[:, g, :].bitcast(FP8X4),
                        rhs_scale=x_scales[:, g, :],
                        start=(g == 0),
                        stop=(g == C_PASSES - 1),
                    )
            lat_banks[n] = lat_bank

        def round_latent(n, engine):
            tile = stage.tile([P, P, R_GROUPS], BF16, name="lat_grouped", tag="lat_grouped", align_bytes=64)
            copy_out = nc.vector.tensor_copy if engine == "v" else nc.scalar.copy
            copy_out(out=tile[:], in_=lat_banks[n][:].rearrange("p t r -> p r t"))
            lat_grouped[n] = tile

        def quantise_latent(n):
            c_tile = stage.tile([P, P], U32, name="lat_codes", tag="lat_codes", align_bytes=64, bufs=4)
            s_tile = stage.tile([P, P], U8, name="lat_scales", tag="lat_scales", align_bytes=64, bufs=4)
            nc.vector.quantize_mx(
                out=c_tile[:].bitcast(FP8X4),
                scales=s_tile[:],
                in_=lat_grouped[n][:].rearrange("p r t -> p (r t)"),
            )
            lat_codes[n], lat_scales[n] = c_tile, s_tile

        order = []
        for pair in range(2):
            for chunk in range(CHUNKS):
                for i in (2 * pair, 2 * pair + 1):
                    order.append((i, chunk))
        for i in range(4, TOKEN_TILES):
            for chunk in range(CHUNKS):
                order.append((i, chunk))

        def project(bank, n, kind, chunk):
            unit = (UP, kind, chunk)
            nc.tensor.matmul_mx(
                out=bank,
                lhsT=lat_codes[n][:].bitcast(FP8X4),
                lhsT_scale=lat_scales[n][:],
                rhs=codes[unit][:].rearrange("p b r -> p (b r)").bitcast(FP8X4),
                rhs_scale=scales[unit][:].rearrange("p b r -> p (b r)"),
                start=True,
                stop=True,
            )

        k_tiles, v_tiles, k_stores, pair_products = {}, {}, [], [None]
        all_sumsq = keep.tile([P, len(order), HEADS_PER_BANK], F32, name="all_sumsq")
        all_rstd = keep.tile([P, len(order), HEADS_PER_BANK], F32, name="all_rstd")

        def copy_values(i, chunk, v_bank, engine):
            half = (chunk % 2) * BANK
            copy_out = nc.vector.tensor_copy if engine == "v" else nc.scalar.copy
            copy_out(
                out=v_tiles[i][:, half : half + BANK], in_=v_bank[:]
            )

        def step(i, chunk, values_engine, after_products, after_step):
            if chunk % 2 == 0:
                k_tiles[i] = results.tile([P, 2 * HEADS_PER_BANK, D], F32, name="k_rot", tag="k_rot")
                v_tiles[i] = results.tile([P, 2 * BANK], F32, name="v_sb", tag="v_sb")
            k_bank = psum.tile([P, HEADS_PER_BANK, D], F32, tag="bank")
            project(k_bank[:].rearrange("p h d -> p (h d)"), i, KEYS, chunk)
            v_bank = psum.tile([P, BANK], F32, tag="bank")
            project(v_bank[:], i, VALUES, chunk)

            s = order.index((i, chunk))
            last = s == len(order) - 1
            single = i == TOKEN_TILES - 1 and chunk >= 2
            stored = single or chunk % 2 == 1
            first = chunk if single else chunk - 1
            columns = slice(first * BANK, (chunk + 1) * BANK)
            part = slice((first % 2) * BANK, (chunk % 2 + 1) * BANK)

            def store_behind_values():
                if stored:
                    nc.sync.dma_start(out=v_out_view[:, i, columns], in_=v_tiles[i][:, part])
                while k_stores and (last or k_stores[0][0] <= s - 2):
                    unused, out, rows = k_stores.pop(0)
                    nc.sync.dma_start(out=out, in_=rows)

            squares = stats.tile([P, HEADS_PER_BANK, D], BF16, tag="squares", bufs=2)
            sumsq, rstd = all_sumsq[:, s, :], all_rstd[:, s, :]
            for h in range(HEADS_PER_BANK):
                nc.scalar.activation(
                    out=squares[:, h, :], in_=k_bank[:, h, :], func=ACT.Square, accum_out=sumsq[:, h : h + 1]
                )
            if values_engine == "s":
                copy_values(i, chunk, v_bank, "s")
                store_behind_values()
            nc.scalar.activation(
                out=rstd, in_=sumsq, func=ACT.Abs_reciprocal_sqrt, scale=1.0 / D, bias=EPS
            )
            if s % 2 == 0:
                pair_products[0] = results.tile(
                    [P, 2, HEADS_PER_BANK, 2, D], F32, name="pair_products", tag="products", bufs=3
                )
            products = pair_products[0][:, s % 2]
            first_head = (chunk % 2) * HEADS_PER_BANK

            def add_products(engine, start, stop):
                engine.tensor_tensor(
                    out=k_tiles[i][:, first_head + start : first_head + stop, :],
                    in0=products[:, start:stop, 0, :],
                    in1=products[:, start:stop, 1, :],
                    op=ALU.add,
                )

            def add_and_store(start, stop):
                add_products(nc.vector, start, stop)
                rows = k_tiles[i][:, first_head + start : first_head + stop, :]
                nc.sync.dma_start(
                    out=k_out_view[:, i, chunk * BANK + start * D : chunk * BANK + stop * D],
                    in_=rows.rearrange("p h d -> p (h d)"),
                )

            for h in range(HEADS_PER_BANK):
                nc.vector.scalar_tensor_tensor(
                    out=products[:, h, :, :].rearrange("p e (j w) -> p (e j) w", w=2),
                    in0=k_bank[:, h, :].unsqueeze(2).to_broadcast([P, D, 2]),
                    scalar=rstd[:, h : h + 1],
                    in1=rope_table[:, i, :, :, :].rearrange("p e j w -> p (e j) w"),
                    op0=ALU.mult,
                    op1=ALU.mult,
                )
                if last and h == 2:
                    add_and_store(0, 2)
            after_products()
            if last:
                add_and_store(2, HEADS_PER_BANK)
            else:
                add_products(nc.gpsimd, 0, HEADS_PER_BANK)
            if stored and not last:
                k_rows = k_tiles[i][:].rearrange("p h d -> p (h d)")
                k_stores.append((s, k_out_view[:, i, columns], k_rows[:, part]))
            if values_engine == "v":
                copy_values(i, chunk, v_bank, "v")
                store_behind_values()
            after_step()

        actions = {}

        def at(s, phase, action):
            actions.setdefault((s, phase), []).append(action)

        for n, unit in enumerate(prologue):
            if n in (10, 12):
                quantise_latent((n - 10) // 2)
            if n > 0:
                quantise(prologue[n - 1])
            transpose(unit, "sv" if n % 2 == 0 else "ss")
            if n == 0:
                make_rope_table()
            if n in (8, 10):
                latent((n - 8) // 2)
                round_latent((n - 8) // 2, "v")
        at(0, "products", lambda: quantise(prologue[-1]))

        def plan_unit(unit, s, engines):
            at(s, "step", lambda: transpose(unit, engines))
            at(s + 1, "products", lambda: quantise(unit))

        def plan_latent(n, s):
            at(s, "step", lambda: latent(n))
            at(s, "step", lambda: round_latent(n, "s"))
            at(s + 1, "products", lambda: quantise_latent(n))

        plan_unit(up[3][0], 0, "sv")
        plan_unit(up[3][1], 1, "ss")
        plan_unit(token[3], 2, "sv")
        plan_latent(2, 3)
        plan_latent(3, 5)
        for n in range(4, TOKEN_TILES):
            plan_unit(token[n], 4 * n - 12, "sv")
            plan_latent(n, 4 * n - 5)

        for s, (i, chunk) in enumerate(order):
            step(
                i,
                chunk,
                "s",
                lambda: [action() for action in actions.get((s, "products"), [])],
                lambda: [action() for action in actions.get((s, "step"), [])],
            )
